import numpy as np
import ml_dtypes


def mxq(x, axis, fmt="e4m3"):
    dtype, down = {"e4m3": (ml_dtypes.float8_e4m3fn, 7), "e5m2": (ml_dtypes.float8_e5m2, 14)}[fmt]
    v = np.moveaxis(np.asarray(x, np.float32).astype(ml_dtypes.bfloat16).astype(np.float64), axis, -1)
    blocks = v.reshape(v.shape[:-1] + (-1, 32))
    amax = np.abs(blocks).max(-1, keepdims=True)
    byte = np.maximum(np.where(amax > 0, np.frexp(amax)[1] - 1 + 127, 0) - down, 1)
    scale = np.exp2(byte - 127.0)
    codes = (blocks / scale).astype(np.float32).astype(dtype).astype(np.float64)
    return np.moveaxis((codes * scale).reshape(v.shape), -1, axis)


WIDE = False


def mx_kscale(k):
    if not WIDE:
        return np.ones(k)
    levels = np.array([10, -10, 5, -5, 0])
    if k % 512:
        return np.exp2(np.random.permutation(np.resize(levels, k // 32))).repeat(32)
    a = np.empty((k // 512, 16))
    for p in range(k // 512):
        a[p, :8] = np.random.permutation(np.resize(levels, 8))
        for g in range(8):
            far = levels[np.abs(levels - a[p, g]) >= 10]
            a[p, g + 8] = far[np.random.randint(len(far))]
    return np.exp2(a.ravel()).repeat(32)


BF16 = ml_dtypes.bfloat16


def bf(x):
    return np.asarray(x, np.float32).astype(BF16)


def f64(x):
    return np.asarray(x).astype(np.float64)


B, N, DIN, DH, DOUT = 256, 4, 512, 512, 512
KH = N * DH
KO = N * DOUT
EPS = 1e-5


def elu(v):
    return np.where(v > 0.0, v, np.expm1(np.minimum(v, 0.0)))


def sigmoid(v):
    return 1.0 / (1.0 + np.exp(-v))


def setup_inputs():
    rn = np.random.standard_normal
    s, t = mx_kscale(KH), mx_kscale(KO)
    return {
        "h": bf(elu(rn((B, KH))) * s),
        "x": bf(rn((B, N, DIN)) + 0.5),
        "cW1": bf(rn((KH, KO)) * 1.2 / np.sqrt(KH) / s[:, None] * t),
        "cb1": bf(rn(KO) * 0.3 * t),
        "cW4": bf(rn((KO, KO)) / np.sqrt(KO) / t[:, None]),
        "cb4": bf(rn(KO) * 0.3),
        "cW5": bf(rn((KO, KO)) / np.sqrt(KO) / t[:, None]),
        "cb5": bf(rn(KO) * 0.3),
        "clng": bf(1.0 + 0.2 * rn(KO)),
        "clnb": bf(0.2 * rn(KO)),
    }


def reference(h, x, cW1, cb1, cW4, cb4, cW5, cb5, clng, clnb):
    flat = f64(x).reshape(B, N * DIN)
    e1 = (mxq(f64(h), 1, "e4m3") @ mxq(f64(cW1), 0, "e4m3")) + f64(cb1)
    e1q = mxq(e1, 1, "e4m3")
    g = sigmoid((e1q @ mxq(f64(cW4), 0, "e4m3")) + f64(cb4)) * ((e1q @ mxq(f64(cW5), 0, "e4m3")) + f64(cb5))
    r = flat + g
    c = (r - r.mean(-1, keepdims=True)) * (1.0 / np.sqrt(r.var(-1, keepdims=True) + EPS)) * f64(clng) + f64(clnb)
    c = c.reshape(B, N, DOUT)
    e = np.exp(c - c.max(1, keepdims=True))
    return e / e.sum(1, keepdims=True)

@@ -1,0 +1,408 @@
+from contextlib import ExitStack
+
+import concourse.mybir as mybir
+from concourse.masks import make_identity
+
+FLOPS = 2 * 256 * 2048 * 2048 * 3
+
+BF16 = mybir.dt.bfloat16
+F32 = mybir.dt.float32
+U32 = mybir.dt.uint32
+U8 = mybir.dt.uint8
+FP8X4 = mybir.dt.float8_e4m3fn_x4
+ALU = mybir.AluOpType
+ACT = mybir.ActivationFunctionType
+AXIS = mybir.AxisListType
+
+P = 128
+PACK = 4
+K_PASS = P * PACK
+BATCH = 256
+BATCH_TILES = BATCH // P
+WIDTH = 2048
+PASSES = WIDTH // K_PASS
+VARIABLES = 4
+FEATURES = WIDTH // VARIABLES
+HALF = WIDTH // 2
+SLICES_PER_VARIABLE = FEATURES // P
+SLICES = WIDTH // P
+GROUPS = SLICES_PER_VARIABLE
+EPS = 1e-5
+CB4 = 0
+CB5 = 1
+GAIN = 2
+SHIFT = 3
+SHARE_AFTER_CW1 = 17
+SHARE_AFTER_CW4 = 19
+SHARE_AFTER_CW5 = 12
+FIRST_LAYER_RANGES = ((0, HALF), (HALF, HALF))
+SECOND_LAYER_RANGES = ((0, HALF), (HALF, FEATURES), (HALF + FEATURES, FEATURES))
+
+
+def word_order(dst, src):
+    return (
+        dst.rearrange("p (c i) t -> p c t i", i=4),
+        src.rearrange("p t (c i) -> p c t i", i=4),
+    )
+
+
+def channel_order(dst, src):
+    return (
+        dst.rearrange("p (t m) j -> p m j t", t=PACK),
+        src.rearrange("p j (m t) -> p m j t", t=PACK),
+    )
+
+
+def tile_variableselectionnetwork_pa_kernel(
+    tc, h, x, cW1, cb1, cW4, cb4, cW5, cb5, clng, clnb, out
+):
+    nc = tc.nc
+    x_rows = x.rearrange("b v f -> b (v f)")
+
+    with tc.tile_pool(name="keep", bufs=1) as keep:
+        ident_bf = keep.tile([P, P], BF16)
+        make_identity(nc, ident_bf[:])
+        ident_f32 = keep.tile([P, P], F32)
+        make_identity(nc, ident_f32[:])
+
+        h_codes = keep.tile([P, PASSES, BATCH], U32, align_bytes=64)
+        h_scales = keep.tile([P, PASSES, BATCH], U8, align_bytes=64)
+        e1_codes = keep.tile([P, PASSES, BATCH], U32, align_bytes=64)
+        e1_scales = keep.tile([P, PASSES, BATCH], U8, align_bytes=64)
+        x_sb = [keep.tile([P, WIDTH], BF16, name="x_sb%d" % bt) for bt in range(BATCH_TILES)]
+        r = [keep.tile([P, WIDTH], F32, name="r%d" % bt) for bt in range(BATCH_TILES)]
+        r_sums = keep.tile([P, BATCH_TILES, VARIABLES], F32)
+        minus_shift = keep.tile([P, BATCH_TILES], F32)
+        square_sums = keep.tile([P, BATCH_TILES, VARIABLES], F32)
+
+        vector_cols = keep.tile([P, P], F32)
+
+        cb1_cols = keep.tile([P, PASSES, PACK], BF16)
+
+        def vector_col(i, s):
+            return vector_cols[:, i * SLICES + s : i * SLICES + s + 1]
+
+        with ExitStack() as stream:
+            raw_pool = stream.enter_context(tc.tile_pool(name="raw", bufs=6))
+            grouped_pool = stream.enter_context(tc.tile_pool(name="grouped", bufs=5))
+            codes_pool = stream.enter_context(tc.tile_pool(name="codes", bufs=2))
+            e1_pool = stream.enter_context(tc.tile_pool(name="e1", bufs=1))
+            gate_pool = stream.enter_context(tc.tile_pool(name="gate", bufs=2))
+            gated_pool = stream.enter_context(tc.tile_pool(name="gated", bufs=4))
+            sums = stream.enter_context(tc.psum_pool(name="sums", bufs=4))
+            flips_bf = stream.enter_context(tc.psum_pool(name="flips_bf", bufs=2))
+            flips_f32 = stream.enter_context(tc.psum_pool(name="flips_f32", bufs=2))
+
+            def quantise_h():
+                with tc.tile_pool(name="head", bufs=1) as head:
+                    h_rows = []
+                    for bt in range(BATCH_TILES):
+                        rows = head.tile([P, WIDTH], BF16, name="h_rows%d" % bt)
+                        nc.sync.dma_start(out=rows[:], in_=h[bt * P : (bt + 1) * P, :])
+                        h_rows.append(rows)
+
+                    nc.scalar.dma_start(
+                        out=cb1_cols[:], in_=cb1.rearrange("(g p t) -> p g t", p=P, t=PACK)
+                    )
+                    vector_rows = head.tile([P, P], BF16)
+                    nc.vector.memset(vector_rows[:], 0.0)
+                    for i, vec in enumerate((cb4, cb5, clng, clnb)):
+                        nc.scalar.dma_start(
+                            out=vector_rows[i * SLICES : (i + 1) * SLICES, :],
+                            in_=vec.rearrange("(s p) -> s p", p=P),
+                        )
+
+                    h_grouped = head.tile([P, PASSES, BATCH, PACK], BF16, align_bytes=64)
+                    for g in range(PASSES):
+                        h_flip = flips_f32.tile([P, PACK // 2, BATCH], F32, tag="g_rows")
+                        for u in range(PACK // 2):
+                            for bt in range(BATCH_TILES):
+                                words = h_rows[bt][:].bitcast(F32)
+                                nc.tensor.transpose(
+                                    out=h_flip[:, u, bt * P : (bt + 1) * P],
+                                    in_=words[:, 2 * P * g + u : 2 * P * (g + 1) : 2],
+                                    identity=ident_f32[:],
+                                )
+                        copy_out = nc.vector.tensor_copy if g % 2 == 0 else nc.scalar.copy
+                        copy_out(
+                            out=h_grouped[:, g, :, :].rearrange("p b t -> p (b t)").bitcast(F32),
+                            in_=h_flip[:].rearrange("p u b -> p b u"),
+                        )
+                    nc.vector.quantize_mx(
+                        out=h_codes[:].rearrange("p g b -> p (g b)").bitcast(FP8X4),
+                        scales=h_scales[:].rearrange("p g b -> p (g b)"),
+                        in_=h_grouped[:].rearrange("p g b t -> p (g b t)"),
+                    )
+
+                    vector_flip = flips_bf.tile([P, P], BF16, tag="flip_bf")
+                    nc.tensor.transpose(out=vector_flip[:], in_=vector_rows[:], identity=ident_bf[:])
+                    nc.vector.tensor_copy(out=vector_cols[:], in_=vector_flip[:])
+
+            def quantise_columns(w, first, width, vector_share, channels=False):
+                codes = codes_pool.tile([P, PASSES, width], U32, align_bytes=64, tag="codes")
+                scales = codes_pool.tile([P, PASSES, width], U8, align_bytes=64, tag="scales")
+                w_passes = w.rearrange("(g p t) n -> g p t n", t=PACK, p=P)
+                split = width * vector_share // 32
+                for g in range(PASSES):
+                    raw = raw_pool.tile([P, PACK, width], BF16, tag="raw")
+                    nc.sync.dma_start(out=raw[:], in_=w_passes[g][:, :, first : first + width])
+                    grouped = grouped_pool.tile([P, width, PACK], BF16, align_bytes=64, tag="grouped")
+                    if channels:
+                        m_split = P * vector_share // 32
+                        for c0 in range(0, width, K_PASS):
+                            cols = slice(c0, c0 + K_PASS)
+                            dst, src = channel_order(grouped[:, cols, :], raw[:, :, cols])
+                            nc.vector.tensor_copy(out=dst[:, :m_split], in_=src[:, :m_split])
+                            nc.scalar.copy(out=dst[:, m_split:], in_=src[:, m_split:])
+                    else:
+                        dst, src = word_order(grouped[:, :split, :], raw[:, :, :split])
+                        nc.vector.tensor_copy(out=dst, in_=src)
+                        dst, src = word_order(grouped[:, split:, :], raw[:, :, split:])
+                        nc.scalar.copy(out=dst, in_=src)
+                    nc.vector.quantize_mx(
+                        out=codes[:, g, :].bitcast(FP8X4),
+                        scales=scales[:, g, :],
+                        in_=grouped[:].rearrange("p c t -> p (c t)"),
+                    )
+                return codes, scales
+
+            def products(codes, scales, j0, act_codes, act_scales):
+                accs = [sums.tile([P, BATCH], F32, name="acc%d" % i, tag="acc") for i in range(PACK)]
+                for g in range(PASSES):
+                    for i in range(PACK):
+                        feats = slice((j0 + i) * P, (j0 + i + 1) * P)
+                        nc.tensor.matmul_mx(
+                            out=accs[i][:],
+                            lhsT=codes[:, g, feats].bitcast(FP8X4),
+                            lhsT_scale=scales[:, g, feats],
+                            rhs=act_codes[:, g, :].bitcast(FP8X4),
+                            rhs_scale=act_scales[:, g, :],
+                            start=(g == 0),
+                            stop=(g == PASSES - 1),
+                        )
+                return accs
+
+            e1_bf = e1_pool.tile([P, PASSES, PACK, BATCH], BF16)
+            e1_grouped = e1_pool.tile([P, PASSES, BATCH, PACK], BF16, align_bytes=64)
+            for first, width in FIRST_LAYER_RANGES:
+                codes, scales = quantise_columns(cW1, first, width, SHARE_AFTER_CW1, channels=True)
+                if first == 0:
+                    quantise_h()
+                for j0 in range(0, width // P, PACK):
+                    g2 = (first // P + j0) // PACK
+                    accs = products(codes, scales, j0, h_codes, h_scales)
+                    for t2 in range(PACK):
+                        nc.scalar.activation(
+                            out=e1_bf[:, g2, t2, :],
+                            in_=accs[t2][:],
+                            func=ACT.Identity,
+                            bias=cb1_cols[:, g2, t2 : t2 + 1],
+                            scale=1.0,
+                        )
+                    dst, src = word_order(e1_grouped[:, g2, :, :], e1_bf[:, g2, :, :])
+                    nc.vector.tensor_copy(out=dst, in_=src)
+                    nc.vector.quantize_mx(
+                        out=e1_codes[:, g2, :].bitcast(FP8X4),
+                        scales=e1_scales[:, g2, :],
+                        in_=e1_grouped[:, g2, :, :].rearrange("p b t -> p (b t)"),
+                    )
+
+            for bt in range(BATCH_TILES):
+                nc.sync.dma_start(out=x_sb[bt][:], in_=x_rows[bt * P : (bt + 1) * P, :])
+
+            for first, width in SECOND_LAYER_RANGES:
+                codes, scales = quantise_columns(
+                    cW4, first, width, SHARE_AFTER_CW1 if first == 0 else SHARE_AFTER_CW5
+                )
+                gate = gate_pool.tile([P, HALF // P, BATCH], F32)
+                for j0 in range(0, width // P, PACK):
+                    accs = products(codes, scales, j0, e1_codes, e1_scales)
+                    for i in range(PACK):
+                        nc.scalar.activation(
+                            out=gate[:, j0 + i, :],
+                            in_=accs[i][:],
+                            func=ACT.Sigmoid,
+                            bias=vector_col(CB4, first // P + j0 + i),
+                            scale=1.0,
+                        )
+                if first + width == WIDTH:
+                    warm = gate_pool.tile([P, 1], F32)
+                    nc.scalar.activation(
+                        out=warm[:], in_=ident_f32[:, 0:1], func=ACT.Abs_reciprocal_sqrt, bias=1.0
+                    )
+
+                codes, scales = quantise_columns(cW5, first, width, SHARE_AFTER_CW4)
+                for v_local in range(width // FEATURES):
+                    v = first // FEATURES + v_local
+                    j0 = v_local * SLICES_PER_VARIABLE
+                    accs = products(codes, scales, j0, e1_codes, e1_scales)
+                    g_rows = [
+                        flips_f32.tile([P, FEATURES], F32, name="g_rows%d" % bt, tag="g_rows")
+                        for bt in range(BATCH_TILES)
+                    ]
+                    for i in range(SLICES_PER_VARIABLE):
+                        g_slice = gated_pool.tile([P, BATCH], F32)
+                        nc.vector.scalar_tensor_tensor(
+                            out=g_slice[:],
+                            in0=accs[i][:],
+                            scalar=vector_col(CB5, first // P + j0 + i),
+                            in1=gate[:, j0 + i, :],
+                            op0=ALU.add,
+                            op1=ALU.mult,
+                        )
+                        for bt in range(BATCH_TILES):
+                            nc.tensor.transpose(
+                                out=g_rows[bt][:, i * P : (i + 1) * P],
+                                in_=g_slice[:, bt * P : (bt + 1) * P],
+                                identity=ident_f32[:],
+                            )
+                    v_cols = slice(v * FEATURES, (v + 1) * FEATURES)
+                    for bt in range(BATCH_TILES):
+                        nc.vector.scalar_tensor_tensor(
+                            out=r[bt][:, v_cols],
+                            in0=g_rows[bt][:],
+                            scalar=1.0,
+                            in1=x_sb[bt][:, v_cols],
+                            op0=ALU.mult,
+                            op1=ALU.add,
+                            accum_out=r_sums[:, bt, v : v + 1],
+                        )
+                        if v == 0:
+                            nc.vector.tensor_scalar_mul(
+                                out=minus_shift[:, bt : bt + 1],
+                                in0=r_sums[:, bt, 0:1],
+                                scalar1=-1.0 / FEATURES,
+                            )
+                        squares = gated_pool.tile([P, FEATURES], BF16)
+                        nc.scalar.activation(
+                            out=squares[:],
+                            in_=r[bt][:, v_cols],
+                            func=ACT.Square,
+                            bias=minus_shift[:, bt : bt + 1],
+                            scale=1.0,
+                            accum_out=square_sums[:, bt, v : v + 1],
+                        )
+
+        with ExitStack() as finish:
+            finish.enter_context(tc.manual_schedule())
+            small = finish.enter_context(tc.tile_pool(name="small", bufs=1))
+            work = finish.enter_context(tc.tile_pool(name="work", bufs=4))
+            per_group = finish.enter_context(tc.tile_pool(name="per_group", bufs=GROUPS))
+            turns = finish.enter_context(tc.psum_pool(name="turns", bufs=8))
+
+            shape = [P, BATCH_TILES]
+            last = VARIABLES - 1
+            total = small.tile(shape, F32)
+            nc.vector.tensor_reduce(out=total[:], in_=r_sums[:], axis=AXIS.X, op=ALU.add)
+            minus_mean = small.tile(shape, F32)
+            nc.vector.tensor_scalar_mul(out=minus_mean[:], in0=total[:], scalar1=-1.0 / WIDTH)
+            offset = small.tile(shape, F32)
+            nc.vector.tensor_sub(out=offset[:], in0=minus_mean[:], in1=minus_shift[:])
+            minus_offset2 = small.tile(shape, F32)
+            nc.vector.scalar_tensor_tensor(
+                out=minus_offset2[:], in0=offset[:], scalar=-1.0, in1=offset[:], op0=ALU.mult, op1=ALU.mult
+            )
+            early = small.tile(shape, F32)
+            nc.vector.tensor_reduce(out=early[:], in_=square_sums[:, :, :last], axis=AXIS.X, op=ALU.add)
+            early_eps = small.tile(shape, F32)
+            nc.vector.tensor_scalar(
+                out=early_eps[:], in0=early[:], scalar1=1.0 / WIDTH, scalar2=EPS, op0=ALU.mult, op1=ALU.add
+            )
+            root_bias = small.tile(shape, F32)
+            nc.vector.tensor_add(out=root_bias[:], in0=early_eps[:], in1=minus_offset2[:])
+            rstd = small.tile(shape, F32)
+            for bt in range(BATCH_TILES):
+                nc.scalar.activation(
+                    out=rstd[:, bt : bt + 1],
+                    in_=square_sums[:, bt, last : last + 1],
+                    func=ACT.Abs_reciprocal_sqrt,
+                    scale=1.0 / WIDTH,
+                    bias=root_bias[:, bt : bt + 1],
+                )
+
+            c_of = []
+            for j in range(GROUPS):
+                z_cols = [
+                    turns.tile([P, 2, BATCH], F32, name="z_cols%d" % pair, tag="turn")
+                    for pair in range(VARIABLES // 2)
+                ]
+                for bt in range(BATCH_TILES):
+                    z = work.tile([P, VARIABLES, P], F32)
+                    nc.vector.tensor_scalar(
+                        out=z[:],
+                        in0=r[bt][:].rearrange("p (v f) -> p v f", v=VARIABLES)[:, :, j * P : (j + 1) * P],
+                        scalar1=minus_mean[:, bt : bt + 1],
+                        scalar2=rstd[:, bt : bt + 1],
+                        op0=ALU.add,
+                        op1=ALU.mult,
+                    )
+                    for v in range(VARIABLES):
+                        nc.tensor.transpose(
+                            out=z_cols[v // 2][:, v % 2, bt * P : (bt + 1) * P],
+                            in_=z[:, v, :],
+                            identity=ident_f32[:],
+                        )
+                c = per_group.tile([P, VARIABLES, BATCH], F32)
+                for v in range(VARIABLES):
+                    s = v * SLICES_PER_VARIABLE + j
+                    nc.scalar.activation(
+                        out=c[:, v, :],
+                        in_=z_cols[v // 2][:, v % 2, :],
+                        func=ACT.Identity,
+                        scale=vector_col(GAIN, s),
+                        bias=vector_col(SHIFT, s),
+                    )
+                c_of.append(c)
+
+            e_rows_of = {}
+            for pair in ((0, 1), (2, 3)):
+                top2_of = {}
+                top_of = {}
+                for j in pair:
+                    top2_of[j] = work.tile([P, 2, BATCH], F32, name="top2")
+                    nc.vector.tensor_max(out=top2_of[j][:], in0=c_of[j][:, 0:2, :], in1=c_of[j][:, 2:4, :])
+                for j in pair:
+                    top_of[j] = work.tile([P, BATCH], F32, name="top")
+                    nc.vector.tensor_max(out=top_of[j][:], in0=top2_of[j][:, 0, :], in1=top2_of[j][:, 1, :])
+                for j in pair:
+                    nc.vector.tensor_sub(
+                        out=c_of[j][:],
+                        in0=c_of[j][:],
+                        in1=top_of[j][:].unsqueeze(1).to_broadcast([P, VARIABLES, BATCH]),
+                    )
+                    nc.scalar.activation(out=c_of[j][:], in_=c_of[j][:], func=ACT.Exp)
+                    for bt in range(BATCH_TILES):
+                        e_rows = turns.tile([P, VARIABLES, P], F32, tag="turn")
+                        for v in range(VARIABLES):
+                            nc.tensor.transpose(
+                                out=e_rows[:, v, :],
+                                in_=c_of[j][:, v, bt * P : (bt + 1) * P],
+                                identity=ident_f32[:],
+                            )
+                        e_rows_of[(j, bt)] = e_rows
+
+            inv_of = []
+            for j in range(GROUPS):
+                inv = per_group.tile([P, BATCH_TILES, P], F32)
+                for bt in range(BATCH_TILES):
+                    nc.vector.tensor_reduce(
+                        out=inv[:, bt, :],
+                        in_=e_rows_of[(j, bt)][:].rearrange("p v f -> p f v"),
+                        axis=AXIS.X,
+                        op=ALU.add,
+                    )
+                nc.scalar.activation(out=inv[:], in_=inv[:], func=ACT.Abs_reciprocal_sqrt)
+                nc.scalar.activation(out=inv[:], in_=inv[:], func=ACT.Square)
+                inv_of.append(inv)
+
+            for j in range(GROUPS):
+                for bt in range(BATCH_TILES):
+                    result = work.tile([P, VARIABLES, P], F32)
+                    nc.vector.tensor_mul(
+                        out=result[:],
+                        in0=e_rows_of[(j, bt)][:],
+                        in1=inv_of[j][:, bt, :].unsqueeze(1).to_broadcast([P, VARIABLES, P]),
+                    )
+                    nc.sync.dma_start(
+                        out=out[bt * P : (bt + 1) * P, :, j * P : (j + 1) * P], in_=result[:]
+                    )

@@ -35,8 +35,11 @@ SHIFT = 3
 SHARE_AFTER_CW1 = 17
 SHARE_AFTER_CW4 = 19
 SHARE_AFTER_CW5 = 12
+SHARE_LAST = 16
 FIRST_LAYER_RANGES = ((0, HALF), (HALF, HALF))
 SECOND_LAYER_RANGES = ((0, HALF), (HALF, FEATURES), (HALF + FEATURES, FEATURES))
+LAST_PARTS = 2
+LAST_CHUNK = VARIABLES - 1 + LAST_PARTS - 1
 
 
 def word_order(dst, src):
@@ -71,9 +74,15 @@ def tile_variableselectionnetwork_pa_kernel(
         e1_scales = keep.tile([P, PASSES, BATCH], U8, align_bytes=64)
         x_sb = [keep.tile([P, WIDTH], BF16, name="x_sb%d" % bt) for bt in range(BATCH_TILES)]
         r = [keep.tile([P, WIDTH], F32, name="r%d" % bt) for bt in range(BATCH_TILES)]
-        r_sums = keep.tile([P, BATCH_TILES, VARIABLES], F32)
+        r_sums = keep.tile([P, BATCH_TILES, LAST_CHUNK + 1], F32)
         minus_shift = keep.tile([P, BATCH_TILES], F32)
-        square_sums = keep.tile([P, BATCH_TILES, VARIABLES], F32)
+        square_sums = keep.tile([P, BATCH_TILES, LAST_CHUNK + 1], F32)
+        early_total = keep.tile([P, BATCH_TILES], F32)
+        early_minus_mean = keep.tile([P, BATCH_TILES], F32)
+        early_offset = keep.tile([P, BATCH_TILES], F32)
+        early_minus_offset = keep.tile([P, BATCH_TILES], F32)
+        early_squares = keep.tile([P, BATCH_TILES], F32)
+        early_variance = keep.tile([P, BATCH_TILES], F32)
 
         vector_cols = keep.tile([P, P], F32)
 
@@ -138,38 +147,51 @@ def tile_variableselectionnetwork_pa_kernel(
                     nc.tensor.transpose(out=vector_flip[:], in_=vector_rows[:], identity=ident_bf[:])
                     nc.vector.tensor_copy(out=vector_cols[:], in_=vector_flip[:])
 
-            def quantise_columns(w, first, width, vector_share, channels=False):
+            def code_tiles(width):
                 codes = codes_pool.tile([P, PASSES, width], U32, align_bytes=64, tag="codes")
                 scales = codes_pool.tile([P, PASSES, width], U8, align_bytes=64, tag="scales")
-                w_passes = w.rearrange("(g p t) n -> g p t n", t=PACK, p=P)
-                split = width * vector_share // 32
-                for g in range(PASSES):
-                    raw = raw_pool.tile([P, PACK, width], BF16, tag="raw")
-                    nc.sync.dma_start(out=raw[:], in_=w_passes[g][:, :, first : first + width])
-                    grouped = grouped_pool.tile([P, width, PACK], BF16, align_bytes=64, tag="grouped")
-                    if channels:
-                        m_split = P * vector_share // 32
-                        for c0 in range(0, width, K_PASS):
-                            cols = slice(c0, c0 + K_PASS)
-                            dst, src = channel_order(grouped[:, cols, :], raw[:, :, cols])
-                            nc.vector.tensor_copy(out=dst[:, :m_split], in_=src[:, :m_split])
-                            nc.scalar.copy(out=dst[:, m_split:], in_=src[:, m_split:])
-                    else:
-                        dst, src = word_order(grouped[:, :split, :], raw[:, :, :split])
-                        nc.vector.tensor_copy(out=dst, in_=src)
-                        dst, src = word_order(grouped[:, split:, :], raw[:, :, split:])
-                        nc.scalar.copy(out=dst, in_=src)
-                    nc.vector.quantize_mx(
-                        out=codes[:, g, :].bitcast(FP8X4),
-                        scales=scales[:, g, :],
-                        in_=grouped[:].rearrange("p c t -> p (c t)"),
-                    )
                 return codes, scales
 
-            def products(codes, scales, j0, act_codes, act_scales):
-                accs = [sums.tile([P, BATCH], F32, name="acc%d" % i, tag="acc") for i in range(PACK)]
+            def load_piece(w, g, first, width):
+                raw = raw_pool.tile([P, PACK, width], BF16, tag="raw")
+                w_passes = w.rearrange("(g p t) n -> g p t n", t=PACK, p=P)
+                nc.sync.dma_start(out=raw[:], in_=w_passes[g][:, :, first : first + width])
+                return raw
+
+            def quantise_piece(raw, codes, scales, g, first, width, vector_share, channels=False):
+                grouped = grouped_pool.tile([P, width, PACK], BF16, align_bytes=64, tag="grouped")
+                src_cols = raw[:, :, first : first + width]
+                if channels:
+                    m_split = P * vector_share // 32
+                    for c0 in range(0, width, K_PASS):
+                        cols = slice(c0, c0 + K_PASS)
+                        dst, src = channel_order(grouped[:, cols, :], src_cols[:, :, cols])
+                        nc.vector.tensor_copy(out=dst[:, :m_split], in_=src[:, :m_split])
+                        nc.scalar.copy(out=dst[:, m_split:], in_=src[:, m_split:])
+                else:
+                    split = width * vector_share // 32
+                    dst, src = word_order(grouped[:, :split, :], src_cols[:, :, :split])
+                    nc.vector.tensor_copy(out=dst, in_=src)
+                    dst, src = word_order(grouped[:, split:, :], src_cols[:, :, split:])
+                    nc.scalar.copy(out=dst, in_=src)
+                nc.vector.quantize_mx(
+                    out=codes[:, g, first : first + width].bitcast(FP8X4),
+                    scales=scales[:, g, first : first + width],
+                    in_=grouped[:].rearrange("p c t -> p (c t)"),
+                )
+                return grouped
+
+            def quantise_columns(w, first, width, vector_share, channels=False):
+                codes, scales = code_tiles(width)
                 for g in range(PASSES):
-                    for i in range(PACK):
+                    raw = load_piece(w, g, first, width)
+                    quantise_piece(raw, codes, scales, g, 0, width, vector_share, channels)
+                return codes, scales
+
+            def products(codes, scales, j0, slices, act_codes, act_scales):
+                accs = [sums.tile([P, BATCH], F32, name="acc%d" % i, tag="acc") for i in range(slices)]
+                for g in range(PASSES):
+                    for i in range(slices):
                         feats = slice((j0 + i) * P, (j0 + i + 1) * P)
                         nc.tensor.matmul_mx(
                             out=accs[i][:],
@@ -182,6 +204,82 @@ def tile_variableselectionnetwork_pa_kernel(
                         )
                 return accs
 
+            def add_chunk(q, codes, scales, gate, range_first, chunk_first, width):
+                j0 = chunk_first // P
+                slices = width // P
+                first = range_first + chunk_first
+                accs = products(codes, scales, j0, slices, e1_codes, e1_scales)
+                g_rows = [
+                    flips_f32.tile([P, width], F32, name="g_rows%d" % bt, tag="g_rows")
+                    for bt in range(BATCH_TILES)
+                ]
+                for i in range(slices):
+                    g_slice = gated_pool.tile([P, BATCH], F32)
+                    nc.vector.scalar_tensor_tensor(
+                        out=g_slice[:],
+                        in0=accs[i][:],
+                        scalar=vector_col(CB5, first // P + i),
+                        in1=gate[:, j0 + i, :],
+                        op0=ALU.add,
+                        op1=ALU.mult,
+                    )
+                    for bt in range(BATCH_TILES):
+                        nc.tensor.transpose(
+                            out=g_rows[bt][:, i * P : (i + 1) * P],
+                            in_=g_slice[:, bt * P : (bt + 1) * P],
+                            identity=ident_f32[:],
+                        )
+                cols = slice(first, first + width)
+                for bt in range(BATCH_TILES):
+                    nc.vector.scalar_tensor_tensor(
+                        out=r[bt][:, cols],
+                        in0=g_rows[bt][:],
+                        scalar=1.0,
+                        in1=x_sb[bt][:, cols],
+                        op0=ALU.mult,
+                        op1=ALU.add,
+                        accum_out=r_sums[:, bt, q : q + 1],
+                    )
+                    if q == 0:
+                        nc.vector.tensor_scalar_mul(
+                            out=minus_shift[:, bt : bt + 1],
+                            in0=r_sums[:, bt, 0:1],
+                            scalar1=-1.0 / width,
+                        )
+                    squares = gated_pool.tile([P, width], BF16)
+                    nc.scalar.activation(
+                        out=squares[:],
+                        in_=r[bt][:, cols],
+                        func=ACT.Square,
+                        bias=minus_shift[:, bt : bt + 1],
+                        scale=1.0,
+                        accum_out=square_sums[:, bt, q : q + 1],
+                    )
+                if q == LAST_CHUNK - 1:
+                    nc.vector.tensor_reduce(
+                        out=early_total[:], in_=r_sums[:, :, :LAST_CHUNK], axis=AXIS.X, op=ALU.add
+                    )
+                    nc.vector.tensor_scalar_mul(
+                        out=early_minus_mean[:], in0=early_total[:], scalar1=-1.0 / WIDTH
+                    )
+                    nc.vector.tensor_sub(
+                        out=early_offset[:], in0=early_minus_mean[:], in1=minus_shift[:]
+                    )
+                    nc.vector.tensor_sub(
+                        out=early_minus_offset[:], in0=minus_shift[:], in1=early_minus_mean[:]
+                    )
+                    nc.vector.tensor_reduce(
+                        out=early_squares[:], in_=square_sums[:, :, :LAST_CHUNK], axis=AXIS.X, op=ALU.add
+                    )
+                    nc.vector.tensor_scalar(
+                        out=early_variance[:],
+                        in0=early_squares[:],
+                        scalar1=1.0 / WIDTH,
+                        scalar2=EPS,
+                        op0=ALU.mult,
+                        op1=ALU.add,
+                    )
+
             e1_bf = e1_pool.tile([P, PASSES, PACK, BATCH], BF16)
             e1_grouped = e1_pool.tile([P, PASSES, BATCH, PACK], BF16, align_bytes=64)
             for first, width in FIRST_LAYER_RANGES:
@@ -190,7 +288,7 @@ def tile_variableselectionnetwork_pa_kernel(
                     quantise_h()
                 for j0 in range(0, width // P, PACK):
                     g2 = (first // P + j0) // PACK
-                    accs = products(codes, scales, j0, h_codes, h_scales)
+                    accs = products(codes, scales, j0, PACK, h_codes, h_scales)
                     for t2 in range(PACK):
                         nc.scalar.activation(
                             out=e1_bf[:, g2, t2, :],
@@ -210,13 +308,14 @@ def tile_variableselectionnetwork_pa_kernel(
             for bt in range(BATCH_TILES):
                 nc.sync.dma_start(out=x_sb[bt][:], in_=x_rows[bt * P : (bt + 1) * P, :])
 
+            chunk = 0
             for first, width in SECOND_LAYER_RANGES:
                 codes, scales = quantise_columns(
                     cW4, first, width, SHARE_AFTER_CW1 if first == 0 else SHARE_AFTER_CW5
                 )
                 gate = gate_pool.tile([P, HALF // P, BATCH], F32)
                 for j0 in range(0, width // P, PACK):
-                    accs = products(codes, scales, j0, e1_codes, e1_scales)
+                    accs = products(codes, scales, j0, PACK, e1_codes, e1_scales)
                     for i in range(PACK):
                         nc.scalar.activation(
                             out=gate[:, j0 + i, :],
@@ -225,109 +324,92 @@ def tile_variableselectionnetwork_pa_kernel(
                             bias=vector_col(CB4, first // P + j0 + i),
                             scale=1.0,
                         )
-                if first + width == WIDTH:
-                    warm = gate_pool.tile([P, 1], F32)
-                    nc.scalar.activation(
-                        out=warm[:], in_=ident_f32[:, 0:1], func=ACT.Abs_reciprocal_sqrt, bias=1.0
-                    )
 
-                codes, scales = quantise_columns(cW5, first, width, SHARE_AFTER_CW4)
-                for v_local in range(width // FEATURES):
-                    v = first // FEATURES + v_local
-                    j0 = v_local * SLICES_PER_VARIABLE
-                    accs = products(codes, scales, j0, e1_codes, e1_scales)
-                    g_rows = [
-                        flips_f32.tile([P, FEATURES], F32, name="g_rows%d" % bt, tag="g_rows")
-                        for bt in range(BATCH_TILES)
-                    ]
-                    for i in range(SLICES_PER_VARIABLE):
-                        g_slice = gated_pool.tile([P, BATCH], F32)
-                        nc.vector.scalar_tensor_tensor(
-                            out=g_slice[:],
-                            in0=accs[i][:],
-                            scalar=vector_col(CB5, first // P + j0 + i),
-                            in1=gate[:, j0 + i, :],
-                            op0=ALU.add,
-                            op1=ALU.mult,
+                codes, scales = code_tiles(width)
+                raws = [load_piece(cW5, g, first, width) for g in range(PASSES)]
+                parts = LAST_PARTS if first + width == WIDTH else 1
+                part_width = width // parts
+                for part_first in range(0, width, part_width):
+                    for g in range(PASSES):
+                        grouped = quantise_piece(
+                            raws[g],
+                            codes,
+                            scales,
+                            g,
+                            part_first,
+                            part_width,
+                            SHARE_AFTER_CW4 if parts == 1 else SHARE_LAST,
                         )
-                        for bt in range(BATCH_TILES):
-                            nc.tensor.transpose(
-                                out=g_rows[bt][:, i * P : (i + 1) * P],
-                                in_=g_slice[:, bt * P : (bt + 1) * P],
-                                identity=ident_f32[:],
-                            )
-                    v_cols = slice(v * FEATURES, (v + 1) * FEATURES)
-                    for bt in range(BATCH_TILES):
-                        nc.vector.scalar_tensor_tensor(
-                            out=r[bt][:, v_cols],
-                            in0=g_rows[bt][:],
-                            scalar=1.0,
-                            in1=x_sb[bt][:, v_cols],
-                            op0=ALU.mult,
-                            op1=ALU.add,
-                            accum_out=r_sums[:, bt, v : v + 1],
-                        )
-                        if v == 0:
-                            nc.vector.tensor_scalar_mul(
-                                out=minus_shift[:, bt : bt + 1],
-                                in0=r_sums[:, bt, 0:1],
-                                scalar1=-1.0 / FEATURES,
-                            )
-                        squares = gated_pool.tile([P, FEATURES], BF16)
+                    if first + part_first + part_width == WIDTH:
+                        warm = gate_pool.tile([P, 1], F32)
                         nc.scalar.activation(
-                            out=squares[:],
-                            in_=r[bt][:, v_cols],
-                            func=ACT.Square,
-                            bias=minus_shift[:, bt : bt + 1],
-                            scale=1.0,
-                            accum_out=square_sums[:, bt, v : v + 1],
+                            out=warm[:],
+                            in_=grouped[:, part_width - 1, 0:1],
+                            func=ACT.Abs_reciprocal_sqrt,
+                            scale=0.0,
+                            bias=1.0,
                         )
+                    chunk_width = min(part_width, FEATURES)
+                    for chunk_first in range(part_first, part_first + part_width, chunk_width):
+                        add_chunk(chunk, codes, scales, gate, first, chunk_first, chunk_width)
+                        chunk += 1
 
         with ExitStack() as finish:
             finish.enter_context(tc.manual_schedule())
             small = finish.enter_context(tc.tile_pool(name="small", bufs=1))
             work = finish.enter_context(tc.tile_pool(name="work", bufs=4))
+            normalised = finish.enter_context(tc.tile_pool(name="normalised", bufs=GROUPS * BATCH_TILES))
+            results = finish.enter_context(tc.tile_pool(name="results", bufs=GROUPS * BATCH_TILES))
             per_group = finish.enter_context(tc.tile_pool(name="per_group", bufs=GROUPS))
             turns = finish.enter_context(tc.psum_pool(name="turns", bufs=8))
 
             shape = [P, BATCH_TILES]
-            last = VARIABLES - 1
-            total = small.tile(shape, F32)
-            nc.vector.tensor_reduce(out=total[:], in_=r_sums[:], axis=AXIS.X, op=ALU.add)
             minus_mean = small.tile(shape, F32)
-            nc.vector.tensor_scalar_mul(out=minus_mean[:], in0=total[:], scalar1=-1.0 / WIDTH)
             offset = small.tile(shape, F32)
-            nc.vector.tensor_sub(out=offset[:], in0=minus_mean[:], in1=minus_shift[:])
-            minus_offset2 = small.tile(shape, F32)
-            nc.vector.scalar_tensor_tensor(
-                out=minus_offset2[:], in0=offset[:], scalar=-1.0, in1=offset[:], op0=ALU.mult, op1=ALU.mult
-            )
-            early = small.tile(shape, F32)
-            nc.vector.tensor_reduce(out=early[:], in_=square_sums[:, :, :last], axis=AXIS.X, op=ALU.add)
-            early_eps = small.tile(shape, F32)
-            nc.vector.tensor_scalar(
-                out=early_eps[:], in0=early[:], scalar1=1.0 / WIDTH, scalar2=EPS, op0=ALU.mult, op1=ALU.add
-            )
+            minus_offset = small.tile(shape, F32)
+            for target, sign, early in (
+                (offset, -1.0, early_offset),
+                (minus_offset, 1.0, early_minus_offset),
+                (minus_mean, -1.0, early_minus_mean),
+            ):
+                nc.vector.scalar_tensor_tensor(
+                    out=target[:],
+                    in0=r_sums[:, :, LAST_CHUNK],
+                    scalar=sign / WIDTH,
+                    in1=early[:],
+                    op0=ALU.mult,
+                    op1=ALU.add,
+                )
             root_bias = small.tile(shape, F32)
-            nc.vector.tensor_add(out=root_bias[:], in0=early_eps[:], in1=minus_offset2[:])
             rstd = small.tile(shape, F32)
             for bt in range(BATCH_TILES):
+                col = slice(bt, bt + 1)
+                nc.vector.scalar_tensor_tensor(
+                    out=root_bias[:, col],
+                    in0=offset[:, col],
+                    scalar=minus_offset[:, col],
+                    in1=early_variance[:, col],
+                    op0=ALU.mult,
+                    op1=ALU.add,
+                )
                 nc.scalar.activation(
-                    out=rstd[:, bt : bt + 1],
-                    in_=square_sums[:, bt, last : last + 1],
+                    out=rstd[:, col],
+                    in_=square_sums[:, bt, LAST_CHUNK : LAST_CHUNK + 1],
                     func=ACT.Abs_reciprocal_sqrt,
                     scale=1.0 / WIDTH,
-                    bias=root_bias[:, bt : bt + 1],
+                    bias=root_bias[:, col],
                 )
+            warm_exp = small.tile([P, 1], F32)
+            nc.scalar.activation(out=warm_exp[:], in_=rstd[:, 0:1], func=ACT.Exp, scale=0.0)
 
-            c_of = []
+            z_cols_of = []
             for j in range(GROUPS):
                 z_cols = [
                     turns.tile([P, 2, BATCH], F32, name="z_cols%d" % pair, tag="turn")
                     for pair in range(VARIABLES // 2)
                 ]
                 for bt in range(BATCH_TILES):
-                    z = work.tile([P, VARIABLES, P], F32)
+                    z = normalised.tile([P, VARIABLES, P], F32)
                     nc.vector.tensor_scalar(
                         out=z[:],
                         in0=r[bt][:].rearrange("p (v f) -> p v f", v=VARIABLES)[:, :, j * P : (j + 1) * P],
@@ -342,65 +424,92 @@ def tile_variableselectionnetwork_pa_kernel(
                             in_=z[:, v, :],
                             identity=ident_f32[:],
                         )
-                c = per_group.tile([P, VARIABLES, BATCH], F32)
-                for v in range(VARIABLES):
-                    s = v * SLICES_PER_VARIABLE + j
-                    nc.scalar.activation(
-                        out=c[:, v, :],
-                        in_=z_cols[v // 2][:, v % 2, :],
-                        func=ACT.Identity,
-                        scale=vector_col(GAIN, s),
-                        bias=vector_col(SHIFT, s),
+                z_cols_of.append(z_cols)
+            c_of = []
+            top2_of = []
+            top_of = []
+            minus_top_of = []
+            for j in range(GROUPS + 1):
+                if j < GROUPS:
+                    c = per_group.tile([P, VARIABLES, BATCH], F32)
+                    for v in range(VARIABLES):
+                        s = v * SLICES_PER_VARIABLE + j
+                        nc.scalar.activation(
+                            out=c[:, v, :],
+                            in_=z_cols_of[j][v // 2][:, v % 2, :],
+                            func=ACT.Identity,
+                            scale=vector_col(GAIN, s),
+                            bias=vector_col(SHIFT, s),
+                        )
+                    c_of.append(c)
+                    top2 = work.tile([P, 2, BATCH], F32)
+                    nc.vector.tensor_max(out=top2[:], in0=c[:, 0:2, :], in1=c[:, 2:4, :])
+                    top2_of.append(top2)
+                if j > 0:
+                    minus_top = per_group.tile([P, BATCH], F32)
+                    nc.vector.tensor_scalar_mul(
+                        out=minus_top[:], in0=top_of[j - 1][:], scalar1=-1.0
                     )
-                c_of.append(c)
-
-            e_rows_of = {}
-            for pair in ((0, 1), (2, 3)):
-                top2_of = {}
-                top_of = {}
-                for j in pair:
-                    top2_of[j] = work.tile([P, 2, BATCH], F32, name="top2")
-                    nc.vector.tensor_max(out=top2_of[j][:], in0=c_of[j][:, 0:2, :], in1=c_of[j][:, 2:4, :])
-                for j in pair:
-                    top_of[j] = work.tile([P, BATCH], F32, name="top")
-                    nc.vector.tensor_max(out=top_of[j][:], in0=top2_of[j][:, 0, :], in1=top2_of[j][:, 1, :])
-                for j in pair:
-                    nc.vector.tensor_sub(
-                        out=c_of[j][:],
-                        in0=c_of[j][:],
-                        in1=top_of[j][:].unsqueeze(1).to_broadcast([P, VARIABLES, BATCH]),
+                    minus_top_of.append(minus_top)
+                if j < GROUPS:
+                    top = work.tile([P, BATCH], F32)
+                    nc.vector.tensor_max(
+                        out=top[:], in0=top2_of[j][:, 0, :], in1=top2_of[j][:, 1, :]
                     )
-                    nc.scalar.activation(out=c_of[j][:], in_=c_of[j][:], func=ACT.Exp)
-                    for bt in range(BATCH_TILES):
-                        e_rows = turns.tile([P, VARIABLES, P], F32, tag="turn")
-                        for v in range(VARIABLES):
-                            nc.tensor.transpose(
-                                out=e_rows[:, v, :],
-                                in_=c_of[j][:, v, bt * P : (bt + 1) * P],
-                                identity=ident_f32[:],
-                            )
-                        e_rows_of[(j, bt)] = e_rows
+                    top_of.append(top)
 
+            e_of = []
+            sum2_of = []
+            sum_of = []
             inv_of = []
-            for j in range(GROUPS):
-                inv = per_group.tile([P, BATCH_TILES, P], F32)
-                for bt in range(BATCH_TILES):
-                    nc.vector.tensor_reduce(
-                        out=inv[:, bt, :],
-                        in_=e_rows_of[(j, bt)][:].rearrange("p v f -> p f v"),
-                        axis=AXIS.X,
-                        op=ALU.add,
+            for j in range(GROUPS + 2):
+                if j < GROUPS:
+                    e = per_group.tile([P, BATCH_TILES, VARIABLES, P], F32)
+                    for bt in range(BATCH_TILES):
+                        rows = slice(bt * P, (bt + 1) * P)
+                        below_top = turns.tile([P, VARIABLES, P], F32, tag="turn")
+                        for v in range(VARIABLES):
+                            nc.tensor.matmul(
+                                out=below_top[:, v, :],
+                                lhsT=c_of[j][:, v, rows],
+                                rhs=ident_f32[:],
+                                is_transpose=True,
+                                start=True,
+                                stop=False,
+                            )
+                            nc.tensor.matmul(
+                                out=below_top[:, v, :],
+                                lhsT=minus_top_of[j][:, rows],
+                                rhs=ident_f32[:],
+                                is_transpose=True,
+                                start=False,
+                                stop=True,
+                            )
+                        nc.scalar.activation(out=e[:, bt, :, :], in_=below_top[:], func=ACT.Exp)
+                    e_of.append(e)
+                    sum2 = work.tile([P, BATCH_TILES, 2, P], F32)
+                    nc.vector.tensor_add(out=sum2[:], in0=e[:, :, 0:2, :], in1=e[:, :, 2:4, :])
+                    sum2_of.append(sum2)
+                if 0 <= j - 2:
+                    inv = per_group.tile([P, BATCH_TILES, P], F32)
+                    nc.vector.tensor_mul(out=inv[:], in0=sum_of[j - 2][:], in1=sum_of[j - 2][:])
+                    inv_of.append(inv)
+                if 0 <= j - 1 < GROUPS:
+                    e_sum = work.tile([P, BATCH_TILES, P], F32)
+                    nc.vector.tensor_add(
+                        out=e_sum[:], in0=sum2_of[j - 1][:, :, 0, :], in1=sum2_of[j - 1][:, :, 1, :]
                     )
+                    sum_of.append(e_sum)
+
+            for inv in inv_of:
                 nc.scalar.activation(out=inv[:], in_=inv[:], func=ACT.Abs_reciprocal_sqrt)
-                nc.scalar.activation(out=inv[:], in_=inv[:], func=ACT.Square)
-                inv_of.append(inv)
 
             for j in range(GROUPS):
                 for bt in range(BATCH_TILES):
-                    result = work.tile([P, VARIABLES, P], F32)
+                    result = results.tile([P, VARIABLES, P], F32)
                     nc.vector.tensor_mul(
                         out=result[:],
-                        in0=e_rows_of[(j, bt)][:],
+                        in0=e_of[j][:, bt, :, :],
                         in1=inv_of[j][:, bt, :].unsqueeze(1).to_broadcast([P, VARIABLES, P]),
                     )
                     nc.sync.dma_start(

@@ -428,7 +428,6 @@ def tile_variableselectionnetwork_pa_kernel(
             c_of = []
             top2_of = []
             top_of = []
-            minus_top_of = []
             for j in range(GROUPS + 1):
                 if j < GROUPS:
                     c = per_group.tile([P, VARIABLES, BATCH], F32)
@@ -446,11 +445,11 @@ def tile_variableselectionnetwork_pa_kernel(
                     nc.vector.tensor_max(out=top2[:], in0=c[:, 0:2, :], in1=c[:, 2:4, :])
                     top2_of.append(top2)
                 if j > 0:
-                    minus_top = per_group.tile([P, BATCH], F32)
-                    nc.vector.tensor_scalar_mul(
-                        out=minus_top[:], in0=top_of[j - 1][:], scalar1=-1.0
+                    nc.vector.tensor_sub(
+                        out=c_of[j - 1][:],
+                        in0=c_of[j - 1][:],
+                        in1=top_of[j - 1][:].unsqueeze(1).to_broadcast([P, VARIABLES, BATCH]),
                     )
-                    minus_top_of.append(minus_top)
                 if j < GROUPS:
                     top = work.tile([P, BATCH], F32)
                     nc.vector.tensor_max(
@@ -458,58 +457,41 @@ def tile_variableselectionnetwork_pa_kernel(
                     )
                     top_of.append(top)
 
-            e_of = []
-            sum2_of = []
-            sum_of = []
-            inv_of = []
-            for j in range(GROUPS + 2):
-                if j < GROUPS:
-                    e = per_group.tile([P, BATCH_TILES, VARIABLES, P], F32)
-                    for bt in range(BATCH_TILES):
-                        rows = slice(bt * P, (bt + 1) * P)
-                        below_top = turns.tile([P, VARIABLES, P], F32, tag="turn")
-                        for v in range(VARIABLES):
-                            nc.tensor.matmul(
-                                out=below_top[:, v, :],
-                                lhsT=c_of[j][:, v, rows],
-                                rhs=ident_f32[:],
-                                is_transpose=True,
-                                start=True,
-                                stop=False,
-                            )
-                            nc.tensor.matmul(
-                                out=below_top[:, v, :],
-                                lhsT=minus_top_of[j][:, rows],
-                                rhs=ident_f32[:],
-                                is_transpose=True,
-                                start=False,
-                                stop=True,
-                            )
-                        nc.scalar.activation(out=e[:, bt, :, :], in_=below_top[:], func=ACT.Exp)
-                    e_of.append(e)
-                    sum2 = work.tile([P, BATCH_TILES, 2, P], F32)
-                    nc.vector.tensor_add(out=sum2[:], in0=e[:, :, 0:2, :], in1=e[:, :, 2:4, :])
-                    sum2_of.append(sum2)
-                if 0 <= j - 2:
-                    inv = per_group.tile([P, BATCH_TILES, P], F32)
-                    nc.vector.tensor_mul(out=inv[:], in0=sum_of[j - 2][:], in1=sum_of[j - 2][:])
-                    inv_of.append(inv)
-                if 0 <= j - 1 < GROUPS:
-                    e_sum = work.tile([P, BATCH_TILES, P], F32)
-                    nc.vector.tensor_add(
-                        out=e_sum[:], in0=sum2_of[j - 1][:, :, 0, :], in1=sum2_of[j - 1][:, :, 1, :]
-                    )
-                    sum_of.append(e_sum)
+            e_rows_of = {}
+            for j in range(GROUPS):
+                nc.scalar.activation(out=c_of[j][:], in_=c_of[j][:], func=ACT.Exp)
+                for bt in range(BATCH_TILES):
+                    e_rows = turns.tile([P, VARIABLES, P], F32, tag="turn")
+                    for v in range(VARIABLES):
+                        nc.tensor.transpose(
+                            out=e_rows[:, v, :],
+                            in_=c_of[j][:, v, bt * P : (bt + 1) * P],
+                            identity=ident_f32[:],
+                        )
+                    e_rows_of[(j, bt)] = e_rows
 
-            for inv in inv_of:
-                nc.scalar.activation(out=inv[:], in_=inv[:], func=ACT.Abs_reciprocal_sqrt)
+            inv_of = []
+            for j in range(GROUPS + 1):
+                if j < GROUPS:
+                    inv = per_group.tile([P, BATCH_TILES, P], F32)
+                    for bt in range(BATCH_TILES):
+                        nc.vector.tensor_reduce(
+                            out=inv[:, bt, :],
+                            in_=e_rows_of[(j, bt)][:].rearrange("p v f -> p f v"),
+                            axis=AXIS.X,
+                            op=ALU.add,
+                        )
+                    nc.scalar.activation(out=inv[:], in_=inv[:], func=ACT.Abs_reciprocal_sqrt)
+                    inv_of.append(inv)
+                if j > 0:
+                    nc.scalar.activation(out=inv_of[j - 1][:], in_=inv_of[j - 1][:], func=ACT.Square)
 
             for j in range(GROUPS):
                 for bt in range(BATCH_TILES):
                     result = results.tile([P, VARIABLES, P], F32)
                     nc.vector.tensor_mul(
                         out=result[:],
-                        in0=e_of[j][:, bt, :, :],
+                        in0=e_rows_of[(j, bt)][:],
                         in1=inv_of[j][:, bt, :].unsqueeze(1).to_broadcast([P, VARIABLES, P]),
                     )
                     nc.sync.dma_start(

@@ -17,6 +17,7 @@ AXIS = mybir.AxisListType
 P = 128
 PACK = 4
 K_PASS = P * PACK
+RUN = 8
 BATCH = 256
 BATCH_TILES = BATCH // P
 WIDTH = 2048
@@ -44,15 +45,15 @@ LAST_CHUNK = VARIABLES - 1 + LAST_PARTS - 1
 
 def word_order(dst, src):
     return (
-        dst.rearrange("p (c i) t -> p c t i", i=4),
-        src.rearrange("p t (c i) -> p c t i", i=4),
+        dst.rearrange("p (c i) t -> p c t i", i=RUN),
+        src.rearrange("p t (c i) -> p c t i", i=RUN),
     )
 
 
 def channel_order(dst, src):
     return (
-        dst.rearrange("p (t m) j -> p m j t", t=PACK),
-        src.rearrange("p j (m t) -> p m j t", t=PACK),
+        dst.rearrange("p (t m i) j -> p m j i t", t=PACK, i=RUN // PACK),
+        src.rearrange("p j (m i t) -> p m j i t", t=PACK, i=RUN // PACK),
     )
 
 
@@ -162,7 +163,7 @@ def tile_variableselectionnetwork_pa_kernel(
                 grouped = grouped_pool.tile([P, width, PACK], BF16, align_bytes=64, tag="grouped")
                 src_cols = raw[:, :, first : first + width]
                 if channels:
-                    m_split = P * vector_share // 32
+                    m_split = P * PACK // RUN * vector_share // 32
                     for c0 in range(0, width, K_PASS):
                         cols = slice(c0, c0 + K_PASS)
                         dst, src = channel_order(grouped[:, cols, :], src_cols[:, :, cols])

@@ -39,7 +39,7 @@ SHARE_AFTER_CW5 = 12
 SHARE_LAST = 16
 FIRST_LAYER_RANGES = ((0, HALF), (HALF, HALF))
 SECOND_LAYER_RANGES = ((0, HALF), (HALF, FEATURES), (HALF + FEATURES, FEATURES))
-LAST_PARTS = 2
+LAST_PARTS = 1
 LAST_CHUNK = VARIABLES - 1 + LAST_PARTS - 1
 
 

@@ -33,9 +33,11 @@ CB4 = 0
 CB5 = 1
 GAIN = 2
 SHIFT = 3
-SHARE_AFTER_CW1 = 17
-SHARE_AFTER_CW4 = 19
-SHARE_AFTER_CW5 = 12
+SHARE_CW1 = 17
+SHARE_AFTER_CW1 = 16
+SHARE_AFTER_CW4 = 18
+SHARE_AFTER_CW5 = 11
+TENSOR_SHARE = 4
 SHARE_LAST = 16
 FIRST_LAYER_RANGES = ((0, HALF), (HALF, HALF))
 SECOND_LAYER_RANGES = ((0, HALF), (HALF, FEATURES), (HALF + FEATURES, FEATURES))
@@ -144,7 +146,7 @@ def tile_variableselectionnetwork_pa_kernel(
                         in_=h_grouped[:].rearrange("p g b t -> p (g b t)"),
                     )
 
-                    vector_flip = flips_bf.tile([P, P], BF16, tag="flip_bf")
+                    vector_flip = flips_bf.tile([P, P], BF16, tag="words")
                     nc.tensor.transpose(out=vector_flip[:], in_=vector_rows[:], identity=ident_bf[:])
                     nc.vector.tensor_copy(out=vector_cols[:], in_=vector_flip[:])
 
@@ -171,10 +173,20 @@ def tile_variableselectionnetwork_pa_kernel(
                         nc.scalar.copy(out=dst[:, m_split:], in_=src[:, m_split:])
                 else:
                     split = width * vector_share // 32
+                    turned = width - width * TENSOR_SHARE // 32
+                    words = flips_bf.tile([P, width - turned, PACK], BF16, tag="words")
+                    nc.tensor.matmul(
+                        out=words[:].rearrange("p c t -> p t c"),
+                        lhsT=ident_bf[:],
+                        rhs=src_cols[:, :, turned:],
+                        start=True,
+                        stop=True,
+                    )
                     dst, src = word_order(grouped[:, :split, :], src_cols[:, :, :split])
                     nc.vector.tensor_copy(out=dst, in_=src)
-                    dst, src = word_order(grouped[:, split:, :], src_cols[:, :, split:])
+                    dst, src = word_order(grouped[:, split:turned, :], src_cols[:, :, split:turned])
                     nc.scalar.copy(out=dst, in_=src)
+                    nc.scalar.copy(out=grouped[:, turned:, :], in_=words[:])
                 nc.vector.quantize_mx(
                     out=codes[:, g, first : first + width].bitcast(FP8X4),
                     scales=scales[:, g, first : first + width],
@@ -284,7 +296,7 @@ def tile_variableselectionnetwork_pa_kernel(
             e1_bf = e1_pool.tile([P, PASSES, PACK, BATCH], BF16)
             e1_grouped = e1_pool.tile([P, PASSES, BATCH, PACK], BF16, align_bytes=64)
             for first, width in FIRST_LAYER_RANGES:
-                codes, scales = quantise_columns(cW1, first, width, SHARE_AFTER_CW1, channels=True)
+                codes, scales = quantise_columns(cW1, first, width, SHARE_CW1, channels=True)
                 if first == 0:
                     quantise_h()
                 for j0 in range(0, width // P, PACK):

@@ -28,6 +28,7 @@ HALF = WIDTH // 2
 SLICES_PER_VARIABLE = FEATURES // P
 SLICES = WIDTH // P
 GROUPS = SLICES_PER_VARIABLE
+VECTOR_GROUP = 2
 EPS = 1e-5
 CB4 = 0
 CB5 = 1
@@ -70,6 +71,10 @@ def tile_variableselectionnetwork_pa_kernel(
         make_identity(nc, ident_bf[:])
         ident_f32 = keep.tile([P, P], F32)
         make_identity(nc, ident_f32[:])
+        minus_ident = keep.tile([P, P], BF16)
+        nc.gpsimd.tensor_scalar(
+            out=minus_ident[:], in0=ident_bf[:], scalar1=-1.0, scalar2=0.0, op0=ALU.mult, op1=ALU.add
+        )
 
         h_codes = keep.tile([P, PASSES, BATCH], U32, align_bytes=64)
         h_scales = keep.tile([P, PASSES, BATCH], U8, align_bytes=64)
@@ -374,7 +379,22 @@ def tile_variableselectionnetwork_pa_kernel(
             normalised = finish.enter_context(tc.tile_pool(name="normalised", bufs=GROUPS * BATCH_TILES))
             results = finish.enter_context(tc.tile_pool(name="results", bufs=GROUPS * BATCH_TILES))
             per_group = finish.enter_context(tc.tile_pool(name="per_group", bufs=GROUPS))
-            turns = finish.enter_context(tc.psum_pool(name="turns", bufs=8))
+            turns = finish.enter_context(tc.psum_pool(name="turns", bufs=7))
+            warmth = finish.enter_context(tc.psum_pool(name="warmth", bufs=1))
+
+            unread = warmth.tile([P, FEATURES], F32)
+
+            def keep_warm(count):
+                for step in range(count):
+                    nc.tensor.matmul(
+                        out=unread[:],
+                        lhsT=ident_bf[:],
+                        rhs=x_sb[0][:, :FEATURES],
+                        start=True,
+                        stop=True,
+                    )
+
+            keep_warm(6)
 
             shape = [P, BATCH_TILES]
             minus_mean = small.tile(shape, F32)
@@ -437,65 +457,114 @@ def tile_variableselectionnetwork_pa_kernel(
                             in_=z[:, v, :],
                             identity=ident_f32[:],
                         )
+                keep_warm(1)
                 z_cols_of.append(z_cols)
-            c_of = []
-            top2_of = []
-            top_of = []
-            for j in range(GROUPS + 1):
-                if j < GROUPS:
-                    c = per_group.tile([P, VARIABLES, BATCH], F32)
-                    for v in range(VARIABLES):
-                        s = v * SLICES_PER_VARIABLE + j
+            c_of = [per_group.tile([P, VARIABLES, BATCH], F32, name="c") for j in range(GROUPS)]
+            top2_of = [work.tile([P, 2, BATCH], F32, name="top2") for j in range(GROUPS)]
+            top_of = [work.tile([P, BATCH], BF16, name="top") for j in range(GROUPS)]
+            e_of = [
+                per_group.tile([P, BATCH_TILES, VARIABLES, P], F32, name="e") for j in range(GROUPS)
+            ]
+            sum2_of = [
+                work.tile([P, BATCH_TILES, 2, P], F32, name="sum2") for j in range(GROUPS)
+            ]
+            inv_of = [per_group.tile([P, BATCH_TILES, P], F32, name="inv") for j in range(GROUPS)]
+            c_rows_of = {}
+
+            def gain_and_shift(j):
+                for v in range(VARIABLES):
+                    s = v * SLICES_PER_VARIABLE + j
+                    z_v = z_cols_of[j][v // 2][:, v % 2, :]
+                    if j == VECTOR_GROUP:
+                        nc.vector.tensor_scalar(
+                            out=c_of[j][:, v, :],
+                            in0=z_v,
+                            scalar1=vector_col(GAIN, s),
+                            scalar2=vector_col(SHIFT, s),
+                            op0=ALU.mult,
+                            op1=ALU.add,
+                        )
+                    else:
                         nc.scalar.activation(
-                            out=c[:, v, :],
-                            in_=z_cols_of[j][v // 2][:, v % 2, :],
+                            out=c_of[j][:, v, :],
+                            in_=z_v,
                             func=ACT.Identity,
                             scale=vector_col(GAIN, s),
                             bias=vector_col(SHIFT, s),
                         )
-                    c_of.append(c)
-                    top2 = work.tile([P, 2, BATCH], F32)
-                    nc.vector.tensor_max(out=top2[:], in0=c[:, 0:2, :], in1=c[:, 2:4, :])
-                    top2_of.append(top2)
-                if j > 0:
-                    nc.vector.tensor_sub(
-                        out=c_of[j - 1][:],
-                        in0=c_of[j - 1][:],
-                        in1=top_of[j - 1][:].unsqueeze(1).to_broadcast([P, VARIABLES, BATCH]),
-                    )
-                if j < GROUPS:
-                    top = work.tile([P, BATCH], F32)
-                    nc.vector.tensor_max(
-                        out=top[:], in0=top2_of[j][:, 0, :], in1=top2_of[j][:, 1, :]
-                    )
-                    top_of.append(top)
 
-            e_rows_of = {}
-            for j in range(GROUPS):
-                nc.scalar.activation(out=c_of[j][:], in_=c_of[j][:], func=ACT.Exp)
+            def half_tops(j):
+                nc.vector.tensor_max(
+                    out=top2_of[j][:], in0=c_of[j][:, 0:2, :], in1=c_of[j][:, 2:4, :]
+                )
+
+            def tops(j):
+                nc.vector.tensor_max(
+                    out=top_of[j][:], in0=top2_of[j][:, 0, :], in1=top2_of[j][:, 1, :]
+                )
+
+            def turn_c(j):
                 for bt in range(BATCH_TILES):
-                    e_rows = turns.tile([P, VARIABLES, P], F32, tag="turn")
+                    c_rows = turns.tile([P, VARIABLES, P], F32, tag="turn")
                     for v in range(VARIABLES):
-                        nc.tensor.transpose(
-                            out=e_rows[:, v, :],
-                            in_=c_of[j][:, v, bt * P : (bt + 1) * P],
-                            identity=ident_f32[:],
+                        nc.tensor.matmul(
+                            out=c_rows[:, v, :],
+                            lhsT=c_of[j][:, v, bt * P : (bt + 1) * P],
+                            rhs=ident_f32[:],
+                            is_transpose=True,
+                            start=(v == 0),
+                            stop=False,
                         )
-                    e_rows_of[(j, bt)] = e_rows
+                    c_rows_of[(j, bt)] = c_rows
+                for bt in range(BATCH_TILES):
+                    nc.tensor.matmul(
+                        out=c_rows_of[(j, bt)][:],
+                        lhsT=top_of[j][:, bt * P : (bt + 1) * P],
+                        rhs=minus_ident[:].unsqueeze(1).to_broadcast([P, VARIABLES, P]),
+                        start=False,
+                        stop=True,
+                    )
+                keep_warm(1)
 
-            inv_of = []
+            def exponentials(j):
+                for bt in range(BATCH_TILES):
+                    nc.scalar.activation(
+                        out=e_of[j][:, bt, :, :], in_=c_rows_of[(j, bt)][:], func=ACT.Exp
+                    )
+
+            def half_sums(j):
+                nc.vector.tensor_add(
+                    out=sum2_of[j][:], in0=e_of[j][:, :, 0:2, :], in1=e_of[j][:, :, 2:4, :]
+                )
+
+            def sums(j):
+                nc.vector.tensor_add(
+                    out=inv_of[j][:], in0=sum2_of[j][:, :, 0, :], in1=sum2_of[j][:, :, 1, :]
+                )
+
+            for j in range(GROUPS):
+                if j != VECTOR_GROUP:
+                    gain_and_shift(j)
+            half_tops(0)
+            tops(0)
+            gain_and_shift(VECTOR_GROUP)
+            for j in range(1, GROUPS + 1):
+                if j < GROUPS:
+                    half_tops(j)
+                if j > 1:
+                    tops(j - 1)
+            for j in range(GROUPS):
+                turn_c(j)
+                exponentials(j)
             for j in range(GROUPS + 1):
                 if j < GROUPS:
-                    inv = per_group.tile([P, BATCH_TILES, P], F32)
-                    for bt in range(BATCH_TILES):
-                        nc.vector.tensor_reduce(
-                            out=inv[:, bt, :],
-                            in_=e_rows_of[(j, bt)][:].rearrange("p v f -> p f v"),
-                            axis=AXIS.X,
-                            op=ALU.add,
-                        )
-                    nc.scalar.activation(out=inv[:], in_=inv[:], func=ACT.Abs_reciprocal_sqrt)
-                    inv_of.append(inv)
+                    half_sums(j)
+                if j > 0:
+                    sums(j - 1)
+
+            for j in range(GROUPS + 1):
+                if j < GROUPS:
+                    nc.scalar.activation(out=inv_of[j][:], in_=inv_of[j][:], func=ACT.Abs_reciprocal_sqrt)
                 if j > 0:
                     nc.scalar.activation(out=inv_of[j - 1][:], in_=inv_of[j - 1][:], func=ACT.Square)
 
@@ -504,7 +573,7 @@ def tile_variableselectionnetwork_pa_kernel(
                     result = results.tile([P, VARIABLES, P], F32)
                     nc.vector.tensor_mul(
                         out=result[:],
-                        in0=e_rows_of[(j, bt)][:],
+                        in0=e_of[j][:, bt, :, :],
                         in1=inv_of[j][:, bt, :].unsqueeze(1).to_broadcast([P, VARIABLES, P]),
                     )
                     nc.sync.dma_start(

from contextlib import ExitStack

import concourse.mybir as mybir
from concourse.masks import make_identity

FLOPS = 2 * 256 * 2048 * 2048 * 3

BF16 = mybir.dt.bfloat16
F32 = mybir.dt.float32
U32 = mybir.dt.uint32
U8 = mybir.dt.uint8
FP8X4 = mybir.dt.float8_e4m3fn_x4
ALU = mybir.AluOpType
ACT = mybir.ActivationFunctionType
AXIS = mybir.AxisListType

P = 128
PACK = 4
K_PASS = P * PACK
RUN = 8
BATCH = 256
BATCH_TILES = BATCH // P
WIDTH = 2048
PASSES = WIDTH // K_PASS
VARIABLES = 4
FEATURES = WIDTH // VARIABLES
HALF = WIDTH // 2
SLICES_PER_VARIABLE = FEATURES // P
SLICES = WIDTH // P
GROUPS = SLICES_PER_VARIABLE
VECTOR_GROUP = 2
EPS = 1e-5
CB4 = 0
CB5 = 1
GAIN = 2
SHIFT = 3
SHARE_CW1 = 17
SHARE_AFTER_CW1 = 16
SHARE_AFTER_CW4 = 18
SHARE_AFTER_CW5 = 11
TENSOR_SHARE = 4
SHARE_LAST = 16
FIRST_LAYER_RANGES = ((0, HALF), (HALF, HALF))
SECOND_LAYER_RANGES = ((0, HALF), (HALF, FEATURES), (HALF + FEATURES, FEATURES))
LAST_PARTS = 1
LAST_CHUNK = VARIABLES - 1 + LAST_PARTS - 1


def word_order(dst, src):
    return (
        dst.rearrange("p (c i) t -> p c t i", i=RUN),
        src.rearrange("p t (c i) -> p c t i", i=RUN),
    )


def channel_order(dst, src):
    return (
        dst.rearrange("p (t m i) j -> p m j i t", t=PACK, i=RUN // PACK),
        src.rearrange("p j (m i t) -> p m j i t", t=PACK, i=RUN // PACK),
    )


def tile_variableselectionnetwork_pa_kernel(
    tc, h, x, cW1, cb1, cW4, cb4, cW5, cb5, clng, clnb, out
):
    nc = tc.nc
    x_rows = x.rearrange("b v f -> b (v f)")

    with tc.tile_pool(name="keep", bufs=1) as keep:
        ident_bf = keep.tile([P, P], BF16)
        make_identity(nc, ident_bf[:])
        ident_f32 = keep.tile([P, P], F32)
        make_identity(nc, ident_f32[:])
        minus_ident = keep.tile([P, P], BF16)
        nc.gpsimd.tensor_scalar(
            out=minus_ident[:], in0=ident_bf[:], scalar1=-1.0, scalar2=0.0, op0=ALU.mult, op1=ALU.add
        )

        h_codes = keep.tile([P, PASSES, BATCH], U32, align_bytes=64)
        h_scales = keep.tile([P, PASSES, BATCH], U8, align_bytes=64)
        e1_codes = keep.tile([P, PASSES, BATCH], U32, align_bytes=64)
        e1_scales = keep.tile([P, PASSES, BATCH], U8, align_bytes=64)
        x_sb = [keep.tile([P, WIDTH], BF16, name="x_sb%d" % bt) for bt in range(BATCH_TILES)]
        r = [keep.tile([P, WIDTH], F32, name="r%d" % bt) for bt in range(BATCH_TILES)]
        r_sums = keep.tile([P, BATCH_TILES, LAST_CHUNK + 1], F32)
        minus_shift = keep.tile([P, BATCH_TILES], F32)
        square_sums = keep.tile([P, BATCH_TILES, LAST_CHUNK + 1], F32)
        early_total = keep.tile([P, BATCH_TILES], F32)
        early_minus_mean = keep.tile([P, BATCH_TILES], F32)
        early_offset = keep.tile([P, BATCH_TILES], F32)
        early_minus_offset = keep.tile([P, BATCH_TILES], F32)
        early_squares = keep.tile([P, BATCH_TILES], F32)
        early_variance = keep.tile([P, BATCH_TILES], F32)

        vector_cols = keep.tile([P, P], F32)

        cb1_cols = keep.tile([P, PASSES, PACK], BF16)

        def vector_col(i, s):
            return vector_cols[:, i * SLICES + s : i * SLICES + s + 1]

        with ExitStack() as stream:
            raw_pool = stream.enter_context(tc.tile_pool(name="raw", bufs=6))
            grouped_pool = stream.enter_context(tc.tile_pool(name="grouped", bufs=5))
            codes_pool = stream.enter_context(tc.tile_pool(name="codes", bufs=2))
            e1_pool = stream.enter_context(tc.tile_pool(name="e1", bufs=1))
            gate_pool = stream.enter_context(tc.tile_pool(name="gate", bufs=2))
            gated_pool = stream.enter_context(tc.tile_pool(name="gated", bufs=4))
            sums = stream.enter_context(tc.psum_pool(name="sums", bufs=4))
            flips_bf = stream.enter_context(tc.psum_pool(name="flips_bf", bufs=2))
            flips_f32 = stream.enter_context(tc.psum_pool(name="flips_f32", bufs=2))

            def quantise_h():
                with tc.tile_pool(name="head", bufs=1) as head:
                    h_rows = []
                    for bt in range(BATCH_TILES):
                        rows = head.tile([P, WIDTH], BF16, name="h_rows%d" % bt)
                        nc.sync.dma_start(out=rows[:], in_=h[bt * P : (bt + 1) * P, :])
                        h_rows.append(rows)

                    nc.scalar.dma_start(
                        out=cb1_cols[:], in_=cb1.rearrange("(g p t) -> p g t", p=P, t=PACK)
                    )
                    vector_rows = head.tile([P, P], BF16)
                    nc.vector.memset(vector_rows[:], 0.0)
                    for i, vec in enumerate((cb4, cb5, clng, clnb)):
                        nc.scalar.dma_start(
                            out=vector_rows[i * SLICES : (i + 1) * SLICES, :],
                            in_=vec.rearrange("(s p) -> s p", p=P),
                        )

                    h_grouped = head.tile([P, PASSES, BATCH, PACK], BF16, align_bytes=64)
                    for g in range(PASSES):
                        h_flip = flips_f32.tile([P, PACK // 2, BATCH], F32, tag="g_rows")
                        for u in range(PACK // 2):
                            for bt in range(BATCH_TILES):
                                words = h_rows[bt][:].bitcast(F32)
                                nc.tensor.transpose(
                                    out=h_flip[:, u, bt * P : (bt + 1) * P],
                                    in_=words[:, 2 * P * g + u : 2 * P * (g + 1) : 2],
                                    identity=ident_f32[:],
                                )
                        copy_out = nc.vector.tensor_copy if g % 2 == 0 else nc.scalar.copy
                        copy_out(
                            out=h_grouped[:, g, :, :].rearrange("p b t -> p (b t)").bitcast(F32),
                            in_=h_flip[:].rearrange("p u b -> p b u"),
                        )
                    nc.vector.quantize_mx(
                        out=h_codes[:].rearrange("p g b -> p (g b)").bitcast(FP8X4),
                        scales=h_scales[:].rearrange("p g b -> p (g b)"),
                        in_=h_grouped[:].rearrange("p g b t -> p (g b t)"),
                    )

                    vector_flip = flips_bf.tile([P, P], BF16, tag="words")
                    nc.tensor.transpose(out=vector_flip[:], in_=vector_rows[:], identity=ident_bf[:])
                    nc.vector.tensor_copy(out=vector_cols[:], in_=vector_flip[:])

            def code_tiles(width):
                codes = codes_pool.tile([P, PASSES, width], U32, align_bytes=64, tag="codes")
                scales = codes_pool.tile([P, PASSES, width], U8, align_bytes=64, tag="scales")
                return codes, scales

            def load_piece(w, g, first, width):
                raw = raw_pool.tile([P, PACK, width], BF16, tag="raw")
                w_passes = w.rearrange("(g p t) n -> g p t n", t=PACK, p=P)
                nc.sync.dma_start(out=raw[:], in_=w_passes[g][:, :, first : first + width])
                return raw

            def quantise_piece(raw, codes, scales, g, first, width, vector_share, channels=False):
                grouped = grouped_pool.tile([P, width, PACK], BF16, align_bytes=64, tag="grouped")
                src_cols = raw[:, :, first : first + width]
                if channels:
                    m_split = P * PACK // RUN * vector_share // 32
                    for c0 in range(0, width, K_PASS):
                        cols = slice(c0, c0 + K_PASS)
                        dst, src = channel_order(grouped[:, cols, :], src_cols[:, :, cols])
                        nc.vector.tensor_copy(out=dst[:, :m_split], in_=src[:, :m_split])
                        nc.scalar.copy(out=dst[:, m_split:], in_=src[:, m_split:])
                else:
                    split = width * vector_share // 32
                    turned = width - width * TENSOR_SHARE // 32
                    words = flips_bf.tile([P, width - turned, PACK], BF16, tag="words")
                    nc.tensor.matmul(
                        out=words[:].rearrange("p c t -> p t c"),
                        lhsT=ident_bf[:],
                        rhs=src_cols[:, :, turned:],
                        start=True,
                        stop=True,
                    )
                    dst, src = word_order(grouped[:, :split, :], src_cols[:, :, :split])
                    nc.vector.tensor_copy(out=dst, in_=src)
                    dst, src = word_order(grouped[:, split:turned, :], src_cols[:, :, split:turned])
                    nc.scalar.copy(out=dst, in_=src)
                    nc.scalar.copy(out=grouped[:, turned:, :], in_=words[:])
                nc.vector.quantize_mx(
                    out=codes[:, g, first : first + width].bitcast(FP8X4),
                    scales=scales[:, g, first : first + width],
                    in_=grouped[:].rearrange("p c t -> p (c t)"),
                )
                return grouped

            def quantise_columns(w, first, width, vector_share, channels=False):
                codes, scales = code_tiles(width)
                for g in range(PASSES):
                    raw = load_piece(w, g, first, width)
                    quantise_piece(raw, codes, scales, g, 0, width, vector_share, channels)
                return codes, scales

            def products(codes, scales, j0, slices, act_codes, act_scales):
                accs = [sums.tile([P, BATCH], F32, name="acc%d" % i, tag="acc") for i in range(slices)]
                for g in range(PASSES):
                    for i in range(slices):
                        feats = slice((j0 + i) * P, (j0 + i + 1) * P)
                        nc.tensor.matmul_mx(
                            out=accs[i][:],
                            lhsT=codes[:, g, feats].bitcast(FP8X4),
                            lhsT_scale=scales[:, g, feats],
                            rhs=act_codes[:, g, :].bitcast(FP8X4),
                            rhs_scale=act_scales[:, g, :],
                            start=(g == 0),
                            stop=(g == PASSES - 1),
                        )
                return accs

            def add_chunk(q, codes, scales, gate, range_first, chunk_first, width):
                j0 = chunk_first // P
                slices = width // P
                first = range_first + chunk_first
                accs = products(codes, scales, j0, slices, e1_codes, e1_scales)
                g_rows = [
                    flips_f32.tile([P, width], F32, name="g_rows%d" % bt, tag="g_rows")
                    for bt in range(BATCH_TILES)
                ]
                for i in range(slices):
                    g_slice = gated_pool.tile([P, BATCH], F32)
                    nc.vector.scalar_tensor_tensor(
                        out=g_slice[:],
                        in0=accs[i][:],
                        scalar=vector_col(CB5, first // P + i),
                        in1=gate[:, j0 + i, :],
                        op0=ALU.add,
                        op1=ALU.mult,
                    )
                    for bt in range(BATCH_TILES):
                        nc.tensor.transpose(
                            out=g_rows[bt][:, i * P : (i + 1) * P],
                            in_=g_slice[:, bt * P : (bt + 1) * P],
                            identity=ident_f32[:],
                        )
                cols = slice(first, first + width)
                for bt in range(BATCH_TILES):
                    nc.vector.scalar_tensor_tensor(
                        out=r[bt][:, cols],
                        in0=g_rows[bt][:],
                        scalar=1.0,
                        in1=x_sb[bt][:, cols],
                        op0=ALU.mult,
                        op1=ALU.add,
                        accum_out=r_sums[:, bt, q : q + 1],
                    )
                    if q == 0:
                        nc.vector.tensor_scalar_mul(
                            out=minus_shift[:, bt : bt + 1],
                            in0=r_sums[:, bt, 0:1],
                            scalar1=-1.0 / width,
                        )
                    squares = gated_pool.tile([P, width], BF16)
                    nc.scalar.activation(
                        out=squares[:],
                        in_=r[bt][:, cols],
                        func=ACT.Square,
                        bias=minus_shift[:, bt : bt + 1],
                        scale=1.0,
                        accum_out=square_sums[:, bt, q : q + 1],
                    )
                if q == LAST_CHUNK - 1:
                    nc.vector.tensor_reduce(
                        out=early_total[:], in_=r_sums[:, :, :LAST_CHUNK], axis=AXIS.X, op=ALU.add
                    )
                    nc.vector.tensor_scalar_mul(
                        out=early_minus_mean[:], in0=early_total[:], scalar1=-1.0 / WIDTH
                    )
                    nc.vector.tensor_sub(
                        out=early_offset[:], in0=early_minus_mean[:], in1=minus_shift[:]
                    )
                    nc.vector.tensor_sub(
                        out=early_minus_offset[:], in0=minus_shift[:], in1=early_minus_mean[:]
                    )
                    nc.vector.tensor_reduce(
                        out=early_squares[:], in_=square_sums[:, :, :LAST_CHUNK], axis=AXIS.X, op=ALU.add
                    )
                    nc.vector.tensor_scalar(
                        out=early_variance[:],
                        in0=early_squares[:],
                        scalar1=1.0 / WIDTH,
                        scalar2=EPS,
                        op0=ALU.mult,
                        op1=ALU.add,
                    )

            e1_bf = e1_pool.tile([P, PASSES, PACK, BATCH], BF16)
            e1_grouped = e1_pool.tile([P, PASSES, BATCH, PACK], BF16, align_bytes=64)
            for first, width in FIRST_LAYER_RANGES:
                codes, scales = quantise_columns(cW1, first, width, SHARE_CW1, channels=True)
                if first == 0:
                    quantise_h()
                for j0 in range(0, width // P, PACK):
                    g2 = (first // P + j0) // PACK
                    accs = products(codes, scales, j0, PACK, h_codes, h_scales)
                    for t2 in range(PACK):
                        nc.scalar.activation(
                            out=e1_bf[:, g2, t2, :],
                            in_=accs[t2][:],
                            func=ACT.Identity,
                            bias=cb1_cols[:, g2, t2 : t2 + 1],
                            scale=1.0,
                        )
                    dst, src = word_order(e1_grouped[:, g2, :, :], e1_bf[:, g2, :, :])
                    nc.vector.tensor_copy(out=dst, in_=src)
                    nc.vector.quantize_mx(
                        out=e1_codes[:, g2, :].bitcast(FP8X4),
                        scales=e1_scales[:, g2, :],
                        in_=e1_grouped[:, g2, :, :].rearrange("p b t -> p (b t)"),
                    )

            for bt in range(BATCH_TILES):
                nc.sync.dma_start(out=x_sb[bt][:], in_=x_rows[bt * P : (bt + 1) * P, :])

            chunk = 0
            for first, width in SECOND_LAYER_RANGES:
                codes, scales = quantise_columns(
                    cW4, first, width, SHARE_AFTER_CW1 if first == 0 else SHARE_AFTER_CW5
                )
                gate = gate_pool.tile([P, HALF // P, BATCH], F32)
                for j0 in range(0, width // P, PACK):
                    accs = products(codes, scales, j0, PACK, e1_codes, e1_scales)
                    for i in range(PACK):
                        nc.scalar.activation(
                            out=gate[:, j0 + i, :],
                            in_=accs[i][:],
                            func=ACT.Sigmoid,
                            bias=vector_col(CB4, first // P + j0 + i),
                            scale=1.0,
                        )

                codes, scales = code_tiles(width)
                raws = [load_piece(cW5, g, first, width) for g in range(PASSES)]
                parts = LAST_PARTS if first + width == WIDTH else 1
                part_width = width // parts
                for part_first in range(0, width, part_width):
                    for g in range(PASSES):
                        grouped = quantise_piece(
                            raws[g],
                            codes,
                            scales,
                            g,
                            part_first,
                            part_width,
                            SHARE_AFTER_CW4 if parts == 1 else SHARE_LAST,
                        )
                    if first + part_first + part_width == WIDTH:
                        warm = gate_pool.tile([P, 1], F32)
                        nc.scalar.activation(
                            out=warm[:],
                            in_=grouped[:, part_width - 1, 0:1],
                            func=ACT.Abs_reciprocal_sqrt,
                            scale=0.0,
                            bias=1.0,
                        )
                    chunk_width = min(part_width, FEATURES)
                    for chunk_first in range(part_first, part_first + part_width, chunk_width):
                        add_chunk(chunk, codes, scales, gate, first, chunk_first, chunk_width)
                        chunk += 1

        with ExitStack() as finish:
            finish.enter_context(tc.manual_schedule())
            small = finish.enter_context(tc.tile_pool(name="small", bufs=1))
            work = finish.enter_context(tc.tile_pool(name="work", bufs=4))
            normalised = finish.enter_context(tc.tile_pool(name="normalised", bufs=GROUPS * BATCH_TILES))
            results = finish.enter_context(tc.tile_pool(name="results", bufs=GROUPS * BATCH_TILES))
            per_group = finish.enter_context(tc.tile_pool(name="per_group", bufs=GROUPS))
            turns = finish.enter_context(tc.psum_pool(name="turns", bufs=7))
            warmth = finish.enter_context(tc.psum_pool(name="warmth", bufs=1))

            unread = warmth.tile([P, FEATURES], F32)

            def keep_warm(count):
                for step in range(count):
                    nc.tensor.matmul(
                        out=unread[:],
                        lhsT=ident_bf[:],
                        rhs=x_sb[0][:, :FEATURES],
                        start=True,
                        stop=True,
                    )

            keep_warm(6)

            shape = [P, BATCH_TILES]
            minus_mean = small.tile(shape, F32)
            offset = small.tile(shape, F32)
            minus_offset = small.tile(shape, F32)
            for target, sign, early in (
                (offset, -1.0, early_offset),
                (minus_offset, 1.0, early_minus_offset),
                (minus_mean, -1.0, early_minus_mean),
            ):
                nc.vector.scalar_tensor_tensor(
                    out=target[:],
                    in0=r_sums[:, :, LAST_CHUNK],
                    scalar=sign / WIDTH,
                    in1=early[:],
                    op0=ALU.mult,
                    op1=ALU.add,
                )
            root_bias = small.tile(shape, F32)
            rstd = small.tile(shape, F32)
            for bt in range(BATCH_TILES):
                col = slice(bt, bt + 1)
                nc.vector.scalar_tensor_tensor(
                    out=root_bias[:, col],
                    in0=offset[:, col],
                    scalar=minus_offset[:, col],
                    in1=early_variance[:, col],
                    op0=ALU.mult,
                    op1=ALU.add,
                )
                nc.scalar.activation(
                    out=rstd[:, col],
                    in_=square_sums[:, bt, LAST_CHUNK : LAST_CHUNK + 1],
                    func=ACT.Abs_reciprocal_sqrt,
                    scale=1.0 / WIDTH,
                    bias=root_bias[:, col],
                )
            warm_exp = small.tile([P, 1], F32)
            nc.scalar.activation(out=warm_exp[:], in_=rstd[:, 0:1], func=ACT.Exp, scale=0.0)

            z_cols_of = []
            for j in range(GROUPS):
                z_cols = [
                    turns.tile([P, 2, BATCH], F32, name="z_cols%d" % pair, tag="turn")
                    for pair in range(VARIABLES // 2)
                ]
                for bt in range(BATCH_TILES):
                    z = normalised.tile([P, VARIABLES, P], F32)
                    nc.vector.tensor_scalar(
                        out=z[:],
                        in0=r[bt][:].rearrange("p (v f) -> p v f", v=VARIABLES)[:, :, j * P : (j + 1) * P],
                        scalar1=minus_mean[:, bt : bt + 1],
                        scalar2=rstd[:, bt : bt + 1],
                        op0=ALU.add,
                        op1=ALU.mult,
                    )
                    for v in range(VARIABLES):
                        nc.tensor.transpose(
                            out=z_cols[v // 2][:, v % 2, bt * P : (bt + 1) * P],
                            in_=z[:, v, :],
                            identity=ident_f32[:],
                        )
                keep_warm(1)
                z_cols_of.append(z_cols)
            c_of = [per_group.tile([P, VARIABLES, BATCH], F32, name="c") for j in range(GROUPS)]
            top2_of = [work.tile([P, 2, BATCH], F32, name="top2") for j in range(GROUPS)]
            top_of = [work.tile([P, BATCH], BF16, name="top") for j in range(GROUPS)]
            e_of = [
                per_group.tile([P, BATCH_TILES, VARIABLES, P], F32, name="e") for j in range(GROUPS)
            ]
            sum2_of = [
                work.tile([P, BATCH_TILES, 2, P], F32, name="sum2") for j in range(GROUPS)
            ]
            inv_of = [per_group.tile([P, BATCH_TILES, P], F32, name="inv") for j in range(GROUPS)]
            c_rows_of = {}

            def gain_and_shift(j):
                for v in range(VARIABLES):
                    s = v * SLICES_PER_VARIABLE + j
                    z_v = z_cols_of[j][v // 2][:, v % 2, :]
                    if j == VECTOR_GROUP:
                        nc.vector.tensor_scalar(
                            out=c_of[j][:, v, :],
                            in0=z_v,
                            scalar1=vector_col(GAIN, s),
                            scalar2=vector_col(SHIFT, s),
                            op0=ALU.mult,
                            op1=ALU.add,
                        )
                    else:
                        nc.scalar.activation(
                            out=c_of[j][:, v, :],
                            in_=z_v,
                            func=ACT.Identity,
                            scale=vector_col(GAIN, s),
                            bias=vector_col(SHIFT, s),
                        )

            def half_tops(j):
                nc.vector.tensor_max(
                    out=top2_of[j][:], in0=c_of[j][:, 0:2, :], in1=c_of[j][:, 2:4, :]
                )

            def tops(j):
                nc.vector.tensor_max(
                    out=top_of[j][:], in0=top2_of[j][:, 0, :], in1=top2_of[j][:, 1, :]
                )

            def turn_c(j):
                for bt in range(BATCH_TILES):
                    c_rows = turns.tile([P, VARIABLES, P], F32, tag="turn")
                    for v in range(VARIABLES):
                        nc.tensor.matmul(
                            out=c_rows[:, v, :],
                            lhsT=c_of[j][:, v, bt * P : (bt + 1) * P],
                            rhs=ident_f32[:],
                            is_transpose=True,
                            start=(v == 0),
                            stop=False,
                        )
                    c_rows_of[(j, bt)] = c_rows
                for bt in range(BATCH_TILES):
                    nc.tensor.matmul(
                        out=c_rows_of[(j, bt)][:],
                        lhsT=top_of[j][:, bt * P : (bt + 1) * P],
                        rhs=minus_ident[:].unsqueeze(1).to_broadcast([P, VARIABLES, P]),
                        start=False,
                        stop=True,
                    )
                keep_warm(1)

            def exponentials(j):
                for bt in range(BATCH_TILES):
                    nc.scalar.activation(
                        out=e_of[j][:, bt, :, :], in_=c_rows_of[(j, bt)][:], func=ACT.Exp
                    )

            def half_sums(j):
                nc.vector.tensor_add(
                    out=sum2_of[j][:], in0=e_of[j][:, :, 0:2, :], in1=e_of[j][:, :, 2:4, :]
                )

            def sums(j):
                nc.vector.tensor_add(
                    out=inv_of[j][:], in0=sum2_of[j][:, :, 0, :], in1=sum2_of[j][:, :, 1, :]
                )

            for j in range(GROUPS):
                if j != VECTOR_GROUP:
                    gain_and_shift(j)
            half_tops(0)
            tops(0)
            gain_and_shift(VECTOR_GROUP)
            for j in range(1, GROUPS + 1):
                if j < GROUPS:
                    half_tops(j)
                if j > 1:
                    tops(j - 1)
            for j in range(GROUPS):
                turn_c(j)
                exponentials(j)
            for j in range(GROUPS + 1):
                if j < GROUPS:
                    half_sums(j)
                if j > 0:
                    sums(j - 1)

            for j in range(GROUPS + 1):
                if j < GROUPS:
                    nc.scalar.activation(out=inv_of[j][:], in_=inv_of[j][:], func=ACT.Abs_reciprocal_sqrt)
                if j > 0:
                    nc.scalar.activation(out=inv_of[j - 1][:], in_=inv_of[j - 1][:], func=ACT.Square)

            for j in range(GROUPS):
                for bt in range(BATCH_TILES):
                    result = results.tile([P, VARIABLES, P], F32)
                    nc.vector.tensor_mul(
                        out=result[:],
                        in0=e_of[j][:, bt, :, :],
                        in1=inv_of[j][:, bt, :].unsqueeze(1).to_broadcast([P, VARIABLES, P]),
                    )
                    nc.sync.dma_start(
                        out=out[bt * P : (bt + 1) * P, :, j * P : (j + 1) * P], in_=result[:]
                    )
